import numpy as np
import ml_dtypes


def mxq(x, axis, fmt="e4m3"):
    dtype, down = {"e4m3": (ml_dtypes.float8_e4m3fn, 7), "e5m2": (ml_dtypes.float8_e5m2, 14)}[fmt]
    v = np.moveaxis(np.asarray(x, np.float32).astype(ml_dtypes.bfloat16).astype(np.float64), axis, -1)
    blocks = v.reshape(v.shape[:-1] + (-1, 32))
    amax = np.abs(blocks).max(-1, keepdims=True)
    byte = np.maximum(np.where(amax > 0, np.frexp(amax)[1] - 1 + 127, 0) - down, 1)
    scale = np.exp2(byte - 127.0)
    codes = (blocks / scale).astype(np.float32).astype(dtype).astype(np.float64)
    return np.moveaxis((codes * scale).reshape(v.shape), -1, axis)


WIDE = False


def mx_kscale(k):
    if not WIDE:
        return np.ones(k)
    levels = np.array([10, -10, 5, -5, 0])
    a = np.random.permutation(np.resize(levels, k // 512 * 4)).reshape(k // 512, 4)
    idx = np.arange(k)
    return np.exp2(a[idx // 512, idx % 128 // 32])


BF16 = ml_dtypes.bfloat16


def bf(x):
    return np.asarray(x, np.float32).astype(BF16)


def f64(x):
    return np.asarray(x).astype(np.float64)


E2M1 = np.array([0.0, 0.5, 1.0, 1.5, 2.0, 3.0, 4.0, 6.0, -0.0, -0.5, -1.0, -1.5, -2.0, -3.0, -4.0, -6.0])


def pack_weight(w, fmt):
    k, n = w.shape
    w = f64(bf(w)).reshape(k // 32, 32, n)
    amax = np.abs(w).max(1)
    if fmt == "e4m3":
        byte = np.frexp(amax)[1] - 1 + 127 - 7
    else:
        mant, ex = np.frexp(amax / 6.0)
        byte = np.where(mant > 0.5, ex, ex - 1) + 127
    byte = np.clip(np.where(amax > 0, byte, 1), 1, 254)
    scaled = (w * np.exp2(127.0 - byte)[:, None, :]).reshape(k, n).astype(np.float32)
    by_word = np.ascontiguousarray(scaled.reshape(k // 512, 128, 4, n).transpose(0, 1, 3, 2))
    if fmt == "e4m3":
        words = by_word.astype(ml_dtypes.float8_e4m3fn).view(np.uint8)
    else:
        c = by_word.astype(ml_dtypes.float4_e2m1fn).view(np.uint8) & 0xF
        words = c[..., 0::2] | (c[..., 1::2] << 4)
    return np.ascontiguousarray(words), np.ascontiguousarray(byte.astype(np.uint8).reshape(k // 512, 16, n))


def unpack_weight(words, scales, fmt):
    g, p, n, _ = words.shape
    if fmt == "e4m3":
        vals = np.ascontiguousarray(words).view(ml_dtypes.float8_e4m3fn).astype(np.float64)
    else:
        nib = np.empty((g, p, n, 4), np.uint8)
        nib[..., 0::2] = words & 0xF
        nib[..., 1::2] = words >> 4
        vals = E2M1[nib]
    vals = vals * np.repeat(np.exp2(scales.astype(np.float64) - 127.0), 8, axis=1)[..., None]
    return vals.transpose(0, 1, 3, 2).reshape(g * 512, n)


B, C, W, H = 8, 512, 16, 32
FMT = "e4m3"


def setup_inputs():
    t = mx_kscale(C)
    x1 = bf(np.random.standard_normal((B, W, H, C)) * t)
    x2 = bf(np.random.standard_normal((B, W, H, C)) * t)
    x3 = bf(np.random.standard_normal((B, W, H, C)) * t)
    hat = bf(np.random.standard_normal((B, 3 * C)))
    w2 = np.random.standard_normal((C, C)) / np.sqrt(C) / t[None, :]
    w2_words, w2_scales = pack_weight(np.ascontiguousarray(w2.T), FMT)
    b2 = bf(np.random.standard_normal(C) * 0.1)
    return {"x1": x1,
            "x2": x2,
            "x3": x3,
            "hat": hat,
            "w2_words": w2_words,
            "w2_scales": w2_scales,
            "b2": b2}


def reference(x1, x2, x3, hat, w2_words, w2_scales, b2):
    hs = f64(hat).reshape(-1, 3, C)
    e = np.exp(hs - hs.max(axis=1, keepdims=True))
    bar = e / e.sum(axis=1, keepdims=True)
    g = bar[:, :, None, None, :]
    out = g[:, 0] * f64(x1) + g[:, 1] * f64(x2) + g[:, 2] * f64(x3)
    z = (mxq(out, 3, "e4m3") @ unpack_weight(w2_words, w2_scales, FMT)) + f64(b2)
    return z.transpose(0, 3, 1, 2)

@@ -1,0 +1,229 @@
+from contextlib import ExitStack
+
+import concourse.mybir as mybir
+from concourse.masks import make_identity
+
+F32 = mybir.dt.float32
+BF16 = mybir.dt.bfloat16
+I32 = mybir.dt.int32
+U32 = mybir.dt.uint32
+U8 = mybir.dt.uint8
+FP8X4 = mybir.dt.float8_e4m3fn_x4
+ACT = mybir.ActivationFunctionType
+ALU = mybir.AluOpType
+
+P = 128
+PACK = 4
+BATCH = 8
+POS = 512
+CH = 512
+BRANCHES = 3
+ROWS = POS // P
+PAIRS = 2
+OUT_TILES = CH // P
+STEPS = BATCH * PAIRS
+AHEAD = 2
+
+FLOPS = 2 * BATCH * POS * CH * CH
+
+
+def tile_modelnew_pb_t_kernel(tc, x1, x2, x3, hat, w2_words, w2_scales, b2, out):
+    nc = tc.nc
+    maps = [x.rearrange("b w (g j) c -> b (w g) (j c)", j=ROWS) for x in (x1, x2, x3)]
+    z_dram = out.rearrange("b (t o) w h -> b o t (w h)", o=P)
+
+    with ExitStack() as ctx:
+        ctx.enter_context(tc.manual_schedule())
+        const = ctx.enter_context(tc.tile_pool(name="const", bufs=1))
+        resident = ctx.enter_context(tc.tile_pool(name="resident", bufs=1))
+        sums = ctx.enter_context(tc.tile_pool(name="sums", bufs=3))
+        work = ctx.enter_context(tc.tile_pool(name="work", bufs=2))
+        results = ctx.enter_context(tc.tile_pool(name="results", bufs=4))
+        psum = ctx.enter_context(tc.psum_pool(name="psum", bufs=2))
+
+        ident = const.tile([P, P], F32)
+        make_identity(nc, ident[:])
+        hat_rows = const.tile([P, CH], BF16)
+        nc.vector.memset(hat_rows[:], 0.0)
+        b2_rows = const.tile([P, P], BF16)
+        nc.vector.memset(b2_rows[:], 0.0)
+        w_scales = const.tile([P, CH], U8, align_bytes=64)
+        nc.vector.memset(w_scales[:].bitcast(I32), 0)
+        w_codes = const.tile([P, CH], U32, align_bytes=64)
+
+        nc.scalar.dma_start(
+            out=hat_rows[0 : BATCH * BRANCHES, :],
+            in_=hat.rearrange("b (k c) -> (b k) c", k=BRANCHES),
+        )
+        nc.scalar.dma_start(out=b2_rows[0:OUT_TILES, :], in_=b2.rearrange("(t o) -> t o", o=P))
+        x_sb = {}
+        for b in range(BATCH):
+            for k in range(BRANCHES):
+                x_sb[k, b] = resident.tile([P, ROWS * CH], BF16, name="x%d_b%d" % (k + 1, b))
+                nc.sync.dma_start(out=x_sb[k, b][:], in_=maps[k][b])
+            if b == 0:
+                nc.sync.dma_start(
+                    out=w_codes[:].bitcast(I32),
+                    in_=w2_words[0].rearrange("p n t -> p (n t)").bitcast(I32),
+                )
+                for quad in range(4):
+                    nc.sync.dma_start(
+                        out=w_scales[32 * quad : 32 * quad + 4, :].bitcast(I32),
+                        in_=w2_scales[0, 4 * quad : 4 * quad + 4, :].bitcast(I32),
+                    )
+
+        hat_words = hat_rows[:].bitcast(F32)
+        hat_t = psum.tile([P, PAIRS, P], F32, tag="acc")
+        for u in range(PAIRS):
+            nc.tensor.transpose(hat_t[:, u, :], hat_words[:, u : CH // 2 : PAIRS], ident[:])
+        hat_halves = (
+            hat_t[:]
+            .rearrange("m u r -> m (u r)")
+            .bitcast(BF16)
+            .rearrange("m (u r e) -> m u r e", u=PAIRS, e=2)
+        )
+        logits = const.tile([P, BRANCHES, BATCH, PACK], F32)
+        for u in range(PAIRS):
+            nc.vector.tensor_copy(
+                out=logits[:, :, :, 2 * u : 2 * u + 2],
+                in_=hat_halves[:, u, 0 : BATCH * BRANCHES, :].rearrange(
+                    "m (b k) e -> m k b e", k=BRANCHES
+                ),
+            )
+        flat = logits[:].rearrange("m k b t -> m k (b t)")
+        spread = [P, BRANCHES, BATCH * PACK]
+        top = const.tile([P, BATCH * PACK], F32)
+        nc.vector.tensor_max(top[:], flat[:, 0, :], flat[:, 1, :])
+        nc.vector.tensor_max(top[:], top[:], flat[:, 2, :])
+        nc.vector.tensor_sub(out=flat, in0=flat, in1=top[:].unsqueeze(1).to_broadcast(spread))
+        b2_f32 = const.tile([P, P], F32)
+        nc.vector.tensor_copy(out=b2_f32[:], in_=b2_rows[:])
+        b2_t = psum.tile([P, P], F32, tag="acc")
+        nc.tensor.transpose(b2_t[:], b2_f32[:], ident[:])
+        expd = const.tile([P, BRANCHES, BATCH * PACK], F32)
+        nc.scalar.activation(out=expd[:], in_=flat, func=ACT.Exp)
+        total = const.tile([P, BATCH * PACK], F32)
+        nc.vector.tensor_add(out=total[:], in0=expd[:, 0, :], in1=expd[:, 1, :])
+        nc.vector.tensor_add(out=total[:], in0=total[:], in1=expd[:, 2, :])
+        nc.vector.reciprocal(out=total[:], in_=total[:])
+        gate = const.tile([P, BRANCHES, BATCH, PACK], F32)
+        nc.vector.tensor_mul(
+            out=gate[:].rearrange("m k b t -> m k (b t)"),
+            in0=expd[:],
+            in1=total[:].unsqueeze(1).to_broadcast(spread),
+        )
+        bias = const.tile([P, OUT_TILES], F32)
+        nc.vector.tensor_copy(out=bias[:], in_=b2_t[:, 0:OUT_TILES])
+
+        banks = {}
+        partials = {}
+        planes = {}
+        grouped = {}
+
+        def transpose_map(k, s):
+            b, u = divmod(s, PAIRS)
+            words = x_sb[k, b][:].bitcast(F32)
+            bank = psum.tile([P, ROWS, P], F32, tag="x%dt" % (k + 1))
+            for j in range(ROWS):
+                first = j * (CH // 2) + u
+                nc.tensor.transpose(
+                    bank[:, j, :], words[:, first : (j + 1) * (CH // 2) : PAIRS], ident[:]
+                )
+            banks[k, s] = bank
+
+        def channel_of_pair(k, s, e):
+            halves = banks[k, s][:].rearrange("m j q -> m (j q)").bitcast(BF16)
+            return halves.rearrange("m (n e) -> m n e", e=2)[:, :, e]
+
+        def weight(k, s, e):
+            b, u = divmod(s, PAIRS)
+            t = 2 * u + e
+            return gate[:, k, b, t : t + 1]
+
+        def start_sum(s):
+            partial = sums.tile([P, 2, POS], F32)
+            for e in range(2):
+                nc.scalar.activation(
+                    out=partial[:, e, :],
+                    in_=channel_of_pair(0, s, e),
+                    func=ACT.Copy,
+                    scale=weight(0, s, e),
+                )
+            partials[s] = partial
+
+        def finish_sum(s):
+            b, u = divmod(s, PAIRS)
+            if u == 0:
+                plane = work.tile([P, PACK, POS], BF16)
+                planes[b] = plane
+            partial = partials[s]
+            for e in range(2):
+                nc.vector.scalar_tensor_tensor(
+                    out=partial[:, e, :],
+                    in0=channel_of_pair(1, s, e),
+                    scalar=weight(1, s, e),
+                    in1=partial[:, e, :],
+                    op0=ALU.mult,
+                    op1=ALU.add,
+                )
+            for e in range(2):
+                nc.vector.scalar_tensor_tensor(
+                    out=planes[b][:, 2 * u + e, :],
+                    in0=channel_of_pair(2, s, e),
+                    scalar=weight(2, s, e),
+                    in1=partial[:, e, :],
+                    op0=ALU.mult,
+                    op1=ALU.add,
+                )
+
+        def regroup(b):
+            side_by_side = work.tile([P, POS, PACK], BF16, align_bytes=64)
+            nc.vector.tensor_copy(out=side_by_side[:], in_=planes[b][:].rearrange("m t n -> m n t"))
+            grouped[b] = side_by_side
+
+        def project(b):
+            codes = work.tile([P, POS], U32, align_bytes=64)
+            scales = work.tile([P, POS], U8, align_bytes=64)
+            nc.vector.quantize_mx(
+                out=codes[:].bitcast(FP8X4),
+                scales=scales[:],
+                in_=grouped[b][:].rearrange("m n t -> m (n t)"),
+            )
+            z_sb = results.tile([P, OUT_TILES, POS], F32)
+            for t in range(OUT_TILES):
+                o_cols = slice(t * P, (t + 1) * P)
+                acc = psum.tile([P, POS], F32, tag="acc")
+                nc.tensor.matmul_mx(
+                    out=acc[:],
+                    lhsT=w_codes[:, o_cols].bitcast(FP8X4),
+                    lhsT_scale=w_scales[:, o_cols],
+                    rhs=codes[:].bitcast(FP8X4),
+                    rhs_scale=scales[:],
+                    start=True,
+                    stop=True,
+                )
+                nc.scalar.activation(
+                    out=z_sb[:, t, :].rearrange("o (q j) -> o q j", j=ROWS),
+                    in_=acc[:].rearrange("o (j q) -> o q j", j=ROWS),
+                    func=ACT.Identity,
+                    bias=bias[:, t : t + 1],
+                )
+                nc.sync.dma_start(out=z_dram[b][:, t, :], in_=z_sb[:, t, :])
+
+        for s in range(AHEAD):
+            for k in range(BRANCHES):
+                transpose_map(k, s)
+            start_sum(s)
+        for s in range(STEPS + 1):
+            if s + AHEAD < STEPS:
+                transpose_map(0, s + AHEAD)
+                start_sum(s + AHEAD)
+            if s < STEPS:
+                finish_sum(s)
+            if s + AHEAD < STEPS:
+                transpose_map(1, s + AHEAD)
+                transpose_map(2, s + AHEAD)
+            if s % PAIRS == 0 and s > 0:
+                project(s // PAIRS - 1)
+            if s % PAIRS == 1:
+                regroup(s // PAIRS)

@@ -178,7 +178,14 @@ def tile_modelnew_pb_t_kernel(tc, x1, x2, x3, hat, w2_words, w2_scales, b2, out)
 
         def regroup(b):
             side_by_side = work.tile([P, POS, PACK], BF16, align_bytes=64)
-            nc.vector.tensor_copy(out=side_by_side[:], in_=planes[b][:].rearrange("m t n -> m n t"))
+            nc.gpsimd.tensor_scalar(
+                out=side_by_side[:],
+                in0=planes[b][:].rearrange("m t n -> m n t"),
+                scalar1=1.0,
+                scalar2=0.0,
+                op0=ALU.mult,
+                op1=ALU.add,
+            )
             grouped[b] = side_by_side
 
         def project(b):

@@ -151,11 +151,7 @@ def tile_modelnew_pb_t_kernel(tc, x1, x2, x3, hat, w2_words, w2_scales, b2, out)
                 )
             partials[s] = partial
 
-        def finish_sum(s):
-            b, u = divmod(s, PAIRS)
-            if u == 0:
-                plane = work.tile([P, PACK, POS], BF16)
-                planes[b] = plane
+        def add_second(s):
             partial = partials[s]
             for e in range(2):
                 nc.vector.scalar_tensor_tensor(
@@ -166,6 +162,13 @@ def tile_modelnew_pb_t_kernel(tc, x1, x2, x3, hat, w2_words, w2_scales, b2, out)
                     op0=ALU.mult,
                     op1=ALU.add,
                 )
+
+        def add_third(s):
+            b, u = divmod(s, PAIRS)
+            if u == 0:
+                plane = work.tile([P, PACK, POS], BF16)
+                planes[b] = plane
+            partial = partials[s]
             for e in range(2):
                 nc.vector.scalar_tensor_tensor(
                     out=planes[b][:, 2 * u + e, :],
@@ -221,16 +224,21 @@ def tile_modelnew_pb_t_kernel(tc, x1, x2, x3, hat, w2_words, w2_scales, b2, out)
             for k in range(BRANCHES):
                 transpose_map(k, s)
             start_sum(s)
-        for s in range(STEPS + 1):
-            if s + AHEAD < STEPS:
-                transpose_map(0, s + AHEAD)
-                start_sum(s + AHEAD)
+        for s in range(STEPS + PAIRS):
+            ahead = s + AHEAD
+            second_step = s % PAIRS == 1
+            if ahead < STEPS:
+                transpose_map(0, ahead)
+                start_sum(ahead)
             if s < STEPS:
-                finish_sum(s)
-            if s + AHEAD < STEPS:
-                transpose_map(1, s + AHEAD)
-                transpose_map(2, s + AHEAD)
-            if s % PAIRS == 0 and s > 0:
+                add_second(s)
+            if ahead < STEPS:
+                transpose_map(1, ahead)
+            if second_step and s > PAIRS:
                 project(s // PAIRS - 1)
-            if s % PAIRS == 1:
+            if s < STEPS:
+                add_third(s)
+            if ahead < STEPS:
+                transpose_map(2, ahead)
+            if second_step and s < STEPS:
                 regroup(s // PAIRS)

@@ -11,6 +11,7 @@ U8 = mybir.dt.uint8
 FP8X4 = mybir.dt.float8_e4m3fn_x4
 ACT = mybir.ActivationFunctionType
 ALU = mybir.AluOpType
+AXIS = mybir.AxisListType
 
 P = 128
 PACK = 4
@@ -18,6 +19,7 @@ BATCH = 8
 POS = 512
 CH = 512
 BRANCHES = 3
+HAT_ROWS = BATCH * BRANCHES
 ROWS = POS // P
 PAIRS = 2
 OUT_TILES = CH // P
@@ -44,24 +46,27 @@ def tile_modelnew_pb_t_kernel(tc, x1, x2, x3, hat, w2_words, w2_scales, b2, out)
         ident = const.tile([P, P], F32)
         make_identity(nc, ident[:])
         hat_rows = const.tile([P, CH], BF16)
-        nc.vector.memset(hat_rows[:], 0.0)
+        nc.vector.memset(hat_rows[32:64, :], 0.0)
+        nc.vector.memset(hat_rows[64:128, :], 0.0)
         b2_rows = const.tile([P, P], BF16)
-        nc.vector.memset(b2_rows[:], 0.0)
+        nc.gpsimd.memset(b2_rows[:], 0.0)
         w_scales = const.tile([P, CH], U8, align_bytes=64)
         nc.vector.memset(w_scales[:].bitcast(I32), 0)
         w_codes = const.tile([P, CH], U32, align_bytes=64)
 
-        nc.scalar.dma_start(
-            out=hat_rows[0 : BATCH * BRANCHES, :],
-            in_=hat.rearrange("b (k c) -> (b k) c", k=BRANCHES),
-        )
-        nc.scalar.dma_start(out=b2_rows[0:OUT_TILES, :], in_=b2.rearrange("(t o) -> t o", o=P))
+        hat_dram = hat.rearrange("b (k c) -> (b k) c", k=BRANCHES)
+        nc.sync.dma_start(out=hat_rows[0:HAT_ROWS, :], in_=hat_dram)
+        nc.sync.dma_start(out=hat_rows[HAT_ROWS:32, :], in_=hat_dram[0 : 32 - HAT_ROWS, :])
         x_sb = {}
         for b in range(BATCH):
             for k in range(BRANCHES):
                 x_sb[k, b] = resident.tile([P, ROWS * CH], BF16, name="x%d_b%d" % (k + 1, b))
                 nc.sync.dma_start(out=x_sb[k, b][:], in_=maps[k][b])
             if b == 0:
+                nc.sync.dma_start(
+                    out=b2_rows[0:OUT_TILES, :], in_=b2.rearrange("(t o) -> t o", o=P)
+                )
+            if b == 1:
                 nc.sync.dma_start(
                     out=w_codes[:].bitcast(I32),
                     in_=w2_words[0].rearrange("p n t -> p (n t)").bitcast(I32),
@@ -86,25 +91,23 @@ def tile_modelnew_pb_t_kernel(tc, x1, x2, x3, hat, w2_words, w2_scales, b2, out)
         for u in range(PAIRS):
             nc.vector.tensor_copy(
                 out=logits[:, :, :, 2 * u : 2 * u + 2],
-                in_=hat_halves[:, u, 0 : BATCH * BRANCHES, :].rearrange(
+                in_=hat_halves[:, u, 0:HAT_ROWS, :].rearrange(
                     "m (b k) e -> m k b e", k=BRANCHES
                 ),
             )
         flat = logits[:].rearrange("m k b t -> m k (b t)")
         spread = [P, BRANCHES, BATCH * PACK]
         top = const.tile([P, BATCH * PACK], F32)
-        nc.vector.tensor_max(top[:], flat[:, 0, :], flat[:, 1, :])
-        nc.vector.tensor_max(top[:], top[:], flat[:, 2, :])
+        nc.vector.tensor_reduce(
+            out=top[:], in_=flat.rearrange("m k n -> m n k"), axis=AXIS.X, op=ALU.max
+        )
         nc.vector.tensor_sub(out=flat, in0=flat, in1=top[:].unsqueeze(1).to_broadcast(spread))
-        b2_f32 = const.tile([P, P], F32)
-        nc.vector.tensor_copy(out=b2_f32[:], in_=b2_rows[:])
-        b2_t = psum.tile([P, P], F32, tag="acc")
-        nc.tensor.transpose(b2_t[:], b2_f32[:], ident[:])
         expd = const.tile([P, BRANCHES, BATCH * PACK], F32)
         nc.scalar.activation(out=expd[:], in_=flat, func=ACT.Exp)
         total = const.tile([P, BATCH * PACK], F32)
-        nc.vector.tensor_add(out=total[:], in0=expd[:, 0, :], in1=expd[:, 1, :])
-        nc.vector.tensor_add(out=total[:], in0=total[:], in1=expd[:, 2, :])
+        nc.vector.tensor_reduce(
+            out=total[:], in_=expd[:].rearrange("m k n -> m n k"), axis=AXIS.X, op=ALU.add
+        )
         nc.vector.reciprocal(out=total[:], in_=total[:])
         gate = const.tile([P, BRANCHES, BATCH, PACK], F32)
         nc.vector.tensor_mul(
@@ -112,8 +115,8 @@ def tile_modelnew_pb_t_kernel(tc, x1, x2, x3, hat, w2_words, w2_scales, b2, out)
             in0=expd[:],
             in1=total[:].unsqueeze(1).to_broadcast(spread),
         )
+
         bias = const.tile([P, OUT_TILES], F32)
-        nc.vector.tensor_copy(out=bias[:], in_=b2_t[:, 0:OUT_TILES])
 
         banks = {}
         partials = {}
@@ -181,7 +184,8 @@ def tile_modelnew_pb_t_kernel(tc, x1, x2, x3, hat, w2_words, w2_scales, b2, out)
 
         def regroup(b):
             side_by_side = work.tile([P, POS, PACK], BF16, align_bytes=64)
-            nc.gpsimd.tensor_scalar(
+            copier = nc.vector if b == BATCH - 1 else nc.gpsimd
+            copier.tensor_scalar(
                 out=side_by_side[:],
                 in0=planes[b][:].rearrange("m t n -> m n t"),
                 scalar1=1.0,
@@ -224,6 +228,11 @@ def tile_modelnew_pb_t_kernel(tc, x1, x2, x3, hat, w2_words, w2_scales, b2, out)
             for k in range(BRANCHES):
                 transpose_map(k, s)
             start_sum(s)
+        b2_f32 = const.tile([P, P], F32)
+        nc.gpsimd.tensor_copy(out=b2_f32[:], in_=b2_rows[:])
+        b2_t = psum.tile([P, P], F32, tag="acc")
+        nc.tensor.transpose(b2_t[:], b2_f32[:], ident[:])
+        nc.scalar.copy(out=bias[:], in_=b2_t[:, 0:OUT_TILES])
         for s in range(STEPS + PAIRS):
             ahead = s + AHEAD
             second_step = s % PAIRS == 1

@@ -35,7 +35,6 @@ def tile_modelnew_pb_t_kernel(tc, x1, x2, x3, hat, w2_words, w2_scales, b2, out)
     z_dram = out.rearrange("b (t o) w h -> b o t (w h)", o=P)
 
     with ExitStack() as ctx:
-        ctx.enter_context(tc.manual_schedule())
         const = ctx.enter_context(tc.tile_pool(name="const", bufs=1))
         resident = ctx.enter_context(tc.tile_pool(name="resident", bufs=1))
         sums = ctx.enter_context(tc.tile_pool(name="sums", bufs=3))

@@ -35,6 +35,7 @@ def tile_modelnew_pb_t_kernel(tc, x1, x2, x3, hat, w2_words, w2_scales, b2, out)
     z_dram = out.rearrange("b (t o) w h -> b o t (w h)", o=P)
 
     with ExitStack() as ctx:
+        ctx.enter_context(tc.manual_schedule())
         const = ctx.enter_context(tc.tile_pool(name="const", bufs=1))
         resident = ctx.enter_context(tc.tile_pool(name="resident", bufs=1))
         sums = ctx.enter_context(tc.tile_pool(name="sums", bufs=3))
@@ -54,7 +55,8 @@ def tile_modelnew_pb_t_kernel(tc, x1, x2, x3, hat, w2_words, w2_scales, b2, out)
         w_codes = const.tile([P, CH], U32, align_bytes=64)
 
         hat_dram = hat.rearrange("b (k c) -> (b k) c", k=BRANCHES)
-        nc.sync.dma_start(out=hat_rows[0:HAT_ROWS, :], in_=hat_dram)
+        nc.sync.dma_start(out=hat_rows[0:16, :], in_=hat_dram[0:16, :])
+        nc.sync.dma_start(out=hat_rows[16:HAT_ROWS, :], in_=hat_dram[16:HAT_ROWS, :])
         nc.sync.dma_start(out=hat_rows[HAT_ROWS:32, :], in_=hat_dram[0 : 32 - HAT_ROWS, :])
         x_sb = {}
         for b in range(BATCH):
@@ -86,33 +88,30 @@ def tile_modelnew_pb_t_kernel(tc, x1, x2, x3, hat, w2_words, w2_scales, b2, out)
             .bitcast(BF16)
             .rearrange("m (u r e) -> m u r e", u=PAIRS, e=2)
         )
-        logits = const.tile([P, BRANCHES, BATCH, PACK], F32)
-        for u in range(PAIRS):
-            nc.vector.tensor_copy(
-                out=logits[:, :, :, 2 * u : 2 * u + 2],
-                in_=hat_halves[:, u, 0:HAT_ROWS, :].rearrange(
-                    "m (b k) e -> m k b e", k=BRANCHES
-                ),
-            )
-        flat = logits[:].rearrange("m k b t -> m k (b t)")
-        spread = [P, BRANCHES, BATCH * PACK]
-        top = const.tile([P, BATCH * PACK], F32)
-        nc.vector.tensor_reduce(
-            out=top[:], in_=flat.rearrange("m k n -> m n k"), axis=AXIS.X, op=ALU.max
+        groups = PAIRS * BATCH
+        logits = const.tile([P, groups, BRANCHES, 2], F32)
+        nc.vector.tensor_copy(
+            out=logits[:].rearrange("m (u b) k e -> m u (b k) e", u=PAIRS),
+            in_=hat_halves[:, :, 0:HAT_ROWS, :],
         )
-        nc.vector.tensor_sub(out=flat, in0=flat, in1=top[:].unsqueeze(1).to_broadcast(spread))
-        expd = const.tile([P, BRANCHES, BATCH * PACK], F32)
-        nc.scalar.activation(out=expd[:], in_=flat, func=ACT.Exp)
-        total = const.tile([P, BATCH * PACK], F32)
+        over_branches = [P, groups, BRANCHES, 2]
+        top = const.tile([P, groups, 2], F32)
         nc.vector.tensor_reduce(
-            out=total[:], in_=expd[:].rearrange("m k n -> m n k"), axis=AXIS.X, op=ALU.add
+            out=top[:], in_=logits[:].rearrange("m g k e -> m g e k"), axis=AXIS.X, op=ALU.max
+        )
+        nc.vector.tensor_sub(
+            out=logits[:], in0=logits[:], in1=top[:].unsqueeze(2).to_broadcast(over_branches)
+        )
+        expd = const.tile([P, groups, BRANCHES, 2], F32)
+        nc.scalar.activation(out=expd[:], in_=logits[:], func=ACT.Exp)
+        total = const.tile([P, groups, 2], F32)
+        nc.vector.tensor_reduce(
+            out=total[:], in_=expd[:].rearrange("m g k e -> m g e k"), axis=AXIS.X, op=ALU.add
         )
         nc.vector.reciprocal(out=total[:], in_=total[:])
-        gate = const.tile([P, BRANCHES, BATCH, PACK], F32)
+        gate = const.tile([P, groups, BRANCHES, 2], F32)
         nc.vector.tensor_mul(
-            out=gate[:].rearrange("m k b t -> m k (b t)"),
-            in0=expd[:],
-            in1=total[:].unsqueeze(1).to_broadcast(spread),
+            out=gate[:], in0=expd[:], in1=total[:].unsqueeze(2).to_broadcast(over_branches)
         )
 
         bias = const.tile([P, OUT_TILES], F32)
@@ -139,8 +138,7 @@ def tile_modelnew_pb_t_kernel(tc, x1, x2, x3, hat, w2_words, w2_scales, b2, out)
 
         def weight(k, s, e):
             b, u = divmod(s, PAIRS)
-            t = 2 * u + e
-            return gate[:, k, b, t : t + 1]
+            return gate[:, u * BATCH + b, k, e : e + 1]
 
         def start_sum(s):
             partial = sums.tile([P, 2, POS], F32)

@@ -25,6 +25,9 @@ PAIRS = 2
 OUT_TILES = CH // P
 STEPS = BATCH * PAIRS
 AHEAD = 2
+LAST = BATCH - 1
+HALVES = 2
+HALF = POS // HALVES
 
 FLOPS = 2 * BATCH * POS * CH * CH
 
@@ -62,7 +65,13 @@ def tile_modelnew_pb_t_kernel(tc, x1, x2, x3, hat, w2_words, w2_scales, b2, out)
         for b in range(BATCH):
             for k in range(BRANCHES):
                 x_sb[k, b] = resident.tile([P, ROWS * CH], BF16, name="x%d_b%d" % (k + 1, b))
-                nc.sync.dma_start(out=x_sb[k, b][:], in_=maps[k][b])
+                if b < LAST:
+                    nc.sync.dma_start(out=x_sb[k, b][:], in_=maps[k][b])
+                else:
+                    nc.sync.dma_start(
+                        out=x_sb[k, b][:].rearrange("q (j c) -> q j c", j=ROWS),
+                        in_=(x1, x2, x3)[k][b].rearrange("(j v) h c -> (v h) j c", j=ROWS),
+                    )
             if b == 0:
                 nc.sync.dma_start(
                     out=b2_rows[0:OUT_TILES, :], in_=b2.rearrange("(t o) -> t o", o=P)
@@ -181,8 +190,7 @@ def tile_modelnew_pb_t_kernel(tc, x1, x2, x3, hat, w2_words, w2_scales, b2, out)
 
         def regroup(b):
             side_by_side = work.tile([P, POS, PACK], BF16, align_bytes=64)
-            copier = nc.vector if b == BATCH - 1 else nc.gpsimd
-            copier.tensor_scalar(
+            nc.gpsimd.tensor_scalar(
                 out=side_by_side[:],
                 in0=planes[b][:].rearrange("m t n -> m n t"),
                 scalar1=1.0,
@@ -221,6 +229,55 @@ def tile_modelnew_pb_t_kernel(tc, x1, x2, x3, hat, w2_words, w2_scales, b2, out)
                 )
                 nc.sync.dma_start(out=z_dram[b][:, t, :], in_=z_sb[:, t, :])
 
+        def project_last():
+            b = LAST
+            side_by_side = work.tile([P, POS, PACK], BF16, align_bytes=64)
+            codes = work.tile([P, POS], U32, align_bytes=64)
+            scales = work.tile([P, POS], U8, align_bytes=64)
+            z_sb = results.tile([P, OUT_TILES, POS], F32)
+            halves = [slice(h * HALF, (h + 1) * HALF) for h in range(HALVES)]
+            for cols in halves:
+                nc.vector.tensor_scalar(
+                    out=side_by_side[:, cols, :],
+                    in0=planes[b][:, :, cols].rearrange("m t n -> m n t"),
+                    scalar1=1.0,
+                    scalar2=0.0,
+                    op0=ALU.mult,
+                    op1=ALU.add,
+                )
+            for cols in halves:
+                nc.vector.quantize_mx(
+                    out=codes[:, cols].bitcast(FP8X4),
+                    scales=scales[:, cols],
+                    in_=side_by_side[:, cols, :].rearrange("m n t -> m (n t)"),
+                )
+            for cols in halves:
+                for t in range(OUT_TILES):
+                    o_cols = slice(t * P, (t + 1) * P)
+                    acc = psum.tile([P, HALF], F32, tag=("acc", "x1t", "x2t", "x3t")[t])
+                    nc.tensor.matmul_mx(
+                        out=acc[:],
+                        lhsT=w_codes[:, o_cols].bitcast(FP8X4),
+                        lhsT_scale=w_scales[:, o_cols],
+                        rhs=codes[:, cols].bitcast(FP8X4),
+                        rhs_scale=scales[:, cols],
+                        start=True,
+                        stop=True,
+                    )
+                    if t % 2 == 0:
+                        nc.scalar.activation(
+                            out=z_sb[:, t, cols], in_=acc[:], func=ACT.Identity, bias=bias[:, t : t + 1]
+                        )
+                    else:
+                        nc.vector.tensor_scalar(
+                            out=z_sb[:, t, cols],
+                            in0=acc[:],
+                            scalar1=bias[:, t : t + 1],
+                            scalar2=None,
+                            op0=ALU.add,
+                        )
+                    nc.sync.dma_start(out=z_dram[b][:, t, cols], in_=z_sb[:, t, cols])
+
         for s in range(AHEAD):
             for k in range(BRANCHES):
                 transpose_map(k, s)
@@ -230,7 +287,7 @@ def tile_modelnew_pb_t_kernel(tc, x1, x2, x3, hat, w2_words, w2_scales, b2, out)
         b2_t = psum.tile([P, P], F32, tag="acc")
         nc.tensor.transpose(b2_t[:], b2_f32[:], ident[:])
         nc.scalar.copy(out=bias[:], in_=b2_t[:, 0:OUT_TILES])
-        for s in range(STEPS + PAIRS):
+        for s in range(STEPS):
             ahead = s + AHEAD
             second_step = s % PAIRS == 1
             if ahead < STEPS:
@@ -240,11 +297,12 @@ def tile_modelnew_pb_t_kernel(tc, x1, x2, x3, hat, w2_words, w2_scales, b2, out)
                 add_second(s)
             if ahead < STEPS:
                 transpose_map(1, ahead)
-            if second_step and s > PAIRS:
+            if second_step and PAIRS < s < STEPS:
                 project(s // PAIRS - 1)
             if s < STEPS:
                 add_third(s)
             if ahead < STEPS:
                 transpose_map(2, ahead)
-            if second_step and s < STEPS:
+            if second_step and s < STEPS - 1:
                 regroup(s // PAIRS)
+        project_last()

@@ -28,6 +28,7 @@ AHEAD = 2
 LAST = BATCH - 1
 HALVES = 2
 HALF = POS // HALVES
+WARM_UP = 3
 
 FLOPS = 2 * BATCH * POS * CH * CH
 
@@ -45,6 +46,12 @@ def tile_modelnew_pb_t_kernel(tc, x1, x2, x3, hat, w2_words, w2_scales, b2, out)
         work = ctx.enter_context(tc.tile_pool(name="work", bufs=2))
         results = ctx.enter_context(tc.tile_pool(name="results", bufs=4))
         psum = ctx.enter_context(tc.psum_pool(name="psum", bufs=2))
+
+        zeros = const.tile([P, POS], BF16)
+        nc.vector.memset(zeros[:], 0.0)
+        for i in range(WARM_UP):
+            idle = psum.tile([P, POS], F32, tag="x1t")
+            nc.tensor.matmul(out=idle[:], lhsT=zeros[:, 0:P], rhs=zeros[:], start=True, stop=True)
 
         ident = const.tile([P, P], F32)
         make_identity(nc, ident[:])
@@ -88,40 +95,53 @@ def tile_modelnew_pb_t_kernel(tc, x1, x2, x3, hat, w2_words, w2_scales, b2, out)
                     )
 
         hat_words = hat_rows[:].bitcast(F32)
-        hat_t = psum.tile([P, PAIRS, P], F32, tag="acc")
+        hat_t = psum.tile([P, HAT_ROWS + P], F32, tag="acc")
         for u in range(PAIRS):
-            nc.tensor.transpose(hat_t[:, u, :], hat_words[:, u : CH // 2 : PAIRS], ident[:])
-        hat_halves = (
-            hat_t[:]
-            .rearrange("m u r -> m (u r)")
-            .bitcast(BF16)
-            .rearrange("m (u r e) -> m u r e", u=PAIRS, e=2)
-        )
+            nc.tensor.transpose(
+                hat_t[:, u * HAT_ROWS : u * HAT_ROWS + P], hat_words[:, u : CH // 2 : PAIRS], ident[:]
+            )
         groups = PAIRS * BATCH
-        logits = const.tile([P, groups, BRANCHES, 2], F32)
-        nc.vector.tensor_copy(
-            out=logits[:].rearrange("m (u b) k e -> m u (b k) e", u=PAIRS),
-            in_=hat_halves[:, :, 0:HAT_ROWS, :],
+        raw_logits = (
+            hat_t[:, 0 : PAIRS * HAT_ROWS]
+            .bitcast(BF16)
+            .rearrange("m (g k e) -> m g k e", k=BRANCHES, e=2)
         )
-        over_branches = [P, groups, BRANCHES, 2]
         top = const.tile([P, groups, 2], F32)
-        nc.vector.tensor_reduce(
-            out=top[:], in_=logits[:].rearrange("m g k e -> m g e k"), axis=AXIS.X, op=ALU.max
-        )
-        nc.vector.tensor_sub(
-            out=logits[:], in0=logits[:], in1=top[:].unsqueeze(2).to_broadcast(over_branches)
-        )
+        logits = const.tile([P, groups, BRANCHES, 2], F32)
         expd = const.tile([P, groups, BRANCHES, 2], F32)
-        nc.scalar.activation(out=expd[:], in_=logits[:], func=ACT.Exp)
         total = const.tile([P, groups, 2], F32)
-        nc.vector.tensor_reduce(
-            out=total[:], in_=expd[:].rearrange("m g k e -> m g e k"), axis=AXIS.X, op=ALU.add
-        )
-        nc.vector.reciprocal(out=total[:], in_=total[:])
         gate = const.tile([P, groups, BRANCHES, 2], F32)
-        nc.vector.tensor_mul(
-            out=gate[:], in0=expd[:], in1=total[:].unsqueeze(2).to_broadcast(over_branches)
-        )
+        parts = (slice(0, 1), slice(1, groups))
+
+        def over_branches(per_group, g):
+            return per_group[:, g, :].unsqueeze(2).to_broadcast([P, g.stop - g.start, BRANCHES, 2])
+
+        for g in parts:
+            nc.vector.tensor_reduce(
+                out=top[:, g, :],
+                in_=raw_logits[:, g, :, :].rearrange("m g k e -> m g e k"),
+                axis=AXIS.X,
+                op=ALU.max,
+            )
+        for g in parts:
+            nc.vector.tensor_sub(
+                out=logits[:, g, :, :], in0=raw_logits[:, g, :, :], in1=over_branches(top, g)
+            )
+        for g in parts:
+            nc.scalar.activation(out=expd[:, g, :, :], in_=logits[:, g, :, :], func=ACT.Exp)
+        for g in parts:
+            nc.vector.tensor_reduce(
+                out=total[:, g, :],
+                in_=expd[:, g, :, :].rearrange("m g k e -> m g e k"),
+                axis=AXIS.X,
+                op=ALU.add,
+            )
+        for g in parts:
+            nc.vector.reciprocal(out=total[:, g, :], in_=total[:, g, :])
+        for g in parts:
+            nc.vector.tensor_mul(
+                out=gate[:, g, :, :], in0=expd[:, g, :, :], in1=over_branches(total, g)
+            )
 
         bias = const.tile([P, OUT_TILES], F32)
 

@@ -28,7 +28,6 @@ AHEAD = 2
 LAST = BATCH - 1
 HALVES = 2
 HALF = POS // HALVES
-WARM_UP = 3
 
 FLOPS = 2 * BATCH * POS * CH * CH
 
@@ -46,12 +45,6 @@ def tile_modelnew_pb_t_kernel(tc, x1, x2, x3, hat, w2_words, w2_scales, b2, out)
         work = ctx.enter_context(tc.tile_pool(name="work", bufs=2))
         results = ctx.enter_context(tc.tile_pool(name="results", bufs=4))
         psum = ctx.enter_context(tc.psum_pool(name="psum", bufs=2))
-
-        zeros = const.tile([P, POS], BF16)
-        nc.vector.memset(zeros[:], 0.0)
-        for i in range(WARM_UP):
-            idle = psum.tile([P, POS], F32, tag="x1t")
-            nc.tensor.matmul(out=idle[:], lhsT=zeros[:, 0:P], rhs=zeros[:], start=True, stop=True)
 
         ident = const.tile([P, P], F32)
         make_identity(nc, ident[:])

@@ -41,7 +41,7 @@ def tile_modelnew_pb_t_kernel(tc, x1, x2, x3, hat, w2_words, w2_scales, b2, out)
         ctx.enter_context(tc.manual_schedule())
         const = ctx.enter_context(tc.tile_pool(name="const", bufs=1))
         resident = ctx.enter_context(tc.tile_pool(name="resident", bufs=1))
-        sums = ctx.enter_context(tc.tile_pool(name="sums", bufs=3))
+        sums = ctx.enter_context(tc.tile_pool(name="sums", bufs=4))
         work = ctx.enter_context(tc.tile_pool(name="work", bufs=2))
         results = ctx.enter_context(tc.tile_pool(name="results", bufs=4))
         psum = ctx.enter_context(tc.psum_pool(name="psum", bufs=2))
@@ -291,31 +291,41 @@ def tile_modelnew_pb_t_kernel(tc, x1, x2, x3, hat, w2_words, w2_scales, b2, out)
                         )
                     nc.sync.dma_start(out=z_dram[b][:, t, cols], in_=z_sb[:, t, cols])
 
-        for s in range(AHEAD):
-            for k in range(BRANCHES):
+        for k in range(BRANCHES):
+            for s in range(AHEAD):
                 transpose_map(k, s)
+        for s in range(AHEAD):
             start_sum(s)
         b2_f32 = const.tile([P, P], F32)
         nc.gpsimd.tensor_copy(out=b2_f32[:], in_=b2_rows[:])
         b2_t = psum.tile([P, P], F32, tag="acc")
         nc.tensor.transpose(b2_t[:], b2_f32[:], ident[:])
         nc.scalar.copy(out=bias[:], in_=b2_t[:, 0:OUT_TILES])
-        for s in range(STEPS):
+        def first_half(s):
             ahead = s + AHEAD
-            second_step = s % PAIRS == 1
             if ahead < STEPS:
                 transpose_map(0, ahead)
                 start_sum(ahead)
-            if s < STEPS:
-                add_second(s)
+            add_second(s)
             if ahead < STEPS:
                 transpose_map(1, ahead)
-            if second_step and PAIRS < s < STEPS:
+
+        def second_half(s):
+            ahead = s + AHEAD
+            second_step = s % PAIRS == 1
+            if second_step and s > PAIRS:
                 project(s // PAIRS - 1)
-            if s < STEPS:
-                add_third(s)
+            add_third(s)
             if ahead < STEPS:
                 transpose_map(2, ahead)
             if second_step and s < STEPS - 1:
                 regroup(s // PAIRS)
+
+        for s in range(PAIRS):
+            first_half(s)
+        for s in range(PAIRS):
+            second_half(s)
+        for s in range(PAIRS, STEPS):
+            first_half(s)
+            second_half(s)
         project_last()

@@ -43,7 +43,7 @@ def tile_modelnew_pb_t_kernel(tc, x1, x2, x3, hat, w2_words, w2_scales, b2, out)
         resident = ctx.enter_context(tc.tile_pool(name="resident", bufs=1))
         sums = ctx.enter_context(tc.tile_pool(name="sums", bufs=4))
         work = ctx.enter_context(tc.tile_pool(name="work", bufs=2))
-        results = ctx.enter_context(tc.tile_pool(name="results", bufs=4))
+        results = ctx.enter_context(tc.tile_pool(name="results", bufs=BATCH))
         psum = ctx.enter_context(tc.psum_pool(name="psum", bufs=2))
 
         ident = const.tile([P, P], F32)

@@ -143,63 +143,75 @@ def tile_modelnew_pb_t_kernel(tc, x1, x2, x3, hat, w2_words, w2_scales, b2, out)
         planes = {}
         grouped = {}
 
+        def parts_of(s):
+            b, h = divmod(s, PAIRS)
+            if b < LAST:
+                return [(h, 0, slice(0, POS))]
+            return [(u, u * HALF, slice(h * HALF, (h + 1) * HALF)) for u in range(PAIRS)]
+
         def transpose_map(k, s):
-            b, u = divmod(s, PAIRS)
+            b, h = divmod(s, PAIRS)
             words = x_sb[k, b][:].bitcast(F32)
             bank = psum.tile([P, ROWS, P], F32, tag="x%dt" % (k + 1))
-            for j in range(ROWS):
+            for i in range(ROWS):
+                u, j = (h, i) if b < LAST else (i // 2, h * 2 + i % 2)
                 first = j * (CH // 2) + u
                 nc.tensor.transpose(
-                    bank[:, j, :], words[:, first : (j + 1) * (CH // 2) : PAIRS], ident[:]
+                    bank[:, i, :], words[:, first : (j + 1) * (CH // 2) : PAIRS], ident[:]
                 )
             banks[k, s] = bank
 
-        def channel_of_pair(k, s, e):
+        def channel_of_pair(k, s, e, start, count):
             halves = banks[k, s][:].rearrange("m j q -> m (j q)").bitcast(BF16)
-            return halves.rearrange("m (n e) -> m n e", e=2)[:, :, e]
+            return halves.rearrange("m (n e) -> m n e", e=2)[:, start : start + count, e]
 
-        def weight(k, s, e):
-            b, u = divmod(s, PAIRS)
+        def weight(k, b, u, e):
             return gate[:, u * BATCH + b, k, e : e + 1]
 
         def start_sum(s):
             partial = sums.tile([P, 2, POS], F32)
-            for e in range(2):
-                nc.scalar.activation(
-                    out=partial[:, e, :],
-                    in_=channel_of_pair(0, s, e),
-                    func=ACT.Copy,
-                    scale=weight(0, s, e),
-                )
+            for u, start, cols in parts_of(s):
+                count = cols.stop - cols.start
+                for e in range(2):
+                    nc.scalar.activation(
+                        out=partial[:, e, start : start + count],
+                        in_=channel_of_pair(0, s, e, start, count),
+                        func=ACT.Copy,
+                        scale=weight(0, s // PAIRS, u, e),
+                    )
             partials[s] = partial
 
-        def add_second(s):
+        def add_second(s, part):
             partial = partials[s]
+            u, start, cols = parts_of(s)[part]
+            count = cols.stop - cols.start
             for e in range(2):
                 nc.vector.scalar_tensor_tensor(
-                    out=partial[:, e, :],
-                    in0=channel_of_pair(1, s, e),
-                    scalar=weight(1, s, e),
-                    in1=partial[:, e, :],
+                    out=partial[:, e, start : start + count],
+                    in0=channel_of_pair(1, s, e, start, count),
+                    scalar=weight(1, s // PAIRS, u, e),
+                    in1=partial[:, e, start : start + count],
                     op0=ALU.mult,
                     op1=ALU.add,
                 )
 
         def add_third(s):
-            b, u = divmod(s, PAIRS)
-            if u == 0:
+            b, h = divmod(s, PAIRS)
+            if h == 0:
                 plane = work.tile([P, PACK, POS], BF16)
                 planes[b] = plane
             partial = partials[s]
-            for e in range(2):
-                nc.vector.scalar_tensor_tensor(
-                    out=planes[b][:, 2 * u + e, :],
-                    in0=channel_of_pair(2, s, e),
-                    scalar=weight(2, s, e),
-                    in1=partial[:, e, :],
-                    op0=ALU.mult,
-                    op1=ALU.add,
-                )
+            for u, start, cols in parts_of(s):
+                count = cols.stop - cols.start
+                for e in range(2):
+                    nc.vector.scalar_tensor_tensor(
+                        out=planes[b][:, 2 * u + e, cols],
+                        in0=channel_of_pair(2, s, e, start, count),
+                        scalar=weight(2, b, u, e),
+                        in1=partial[:, e, start : start + count],
+                        op0=ALU.mult,
+                        op1=ALU.add,
+                    )
 
         def regroup(b):
             side_by_side = work.tile([P, POS, PACK], BF16, align_bytes=64)
@@ -213,7 +225,9 @@ def tile_modelnew_pb_t_kernel(tc, x1, x2, x3, hat, w2_words, w2_scales, b2, out)
             )
             grouped[b] = side_by_side
 
-        def project(b):
+        quantised = {}
+
+        def quantise(b):
             codes = work.tile([P, POS], U32, align_bytes=64)
             scales = work.tile([P, POS], U8, align_bytes=64)
             nc.vector.quantize_mx(
@@ -222,9 +236,13 @@ def tile_modelnew_pb_t_kernel(tc, x1, x2, x3, hat, w2_words, w2_scales, b2, out)
                 in_=grouped[b][:].rearrange("m n t -> m (n t)"),
             )
             z_sb = results.tile([P, OUT_TILES, POS], F32)
-            for t in range(OUT_TILES):
+            quantised[b] = (codes, scales, z_sb)
+
+        def project(b, tiles):
+            codes, scales, z_sb = quantised[b]
+            for t in tiles:
                 o_cols = slice(t * P, (t + 1) * P)
-                acc = psum.tile([P, POS], F32, tag="acc")
+                acc = psum.tile([P, POS], F32, tag="x1t" if b == LAST - 1 and t >= 2 else "acc")
                 nc.tensor.matmul_mx(
                     out=acc[:],
                     lhsT=w_codes[:, o_cols].bitcast(FP8X4),
@@ -242,54 +260,69 @@ def tile_modelnew_pb_t_kernel(tc, x1, x2, x3, hat, w2_words, w2_scales, b2, out)
                 )
                 nc.sync.dma_start(out=z_dram[b][:, t, :], in_=z_sb[:, t, :])
 
-        def project_last():
-            b = LAST
-            side_by_side = work.tile([P, POS, PACK], BF16, align_bytes=64)
+        last = {}
+
+        def last_tiles():
+            grouped_last = work.tile([P, POS, PACK], BF16, align_bytes=64)
             codes = work.tile([P, POS], U32, align_bytes=64)
             scales = work.tile([P, POS], U8, align_bytes=64)
             z_sb = results.tile([P, OUT_TILES, POS], F32)
-            halves = [slice(h * HALF, (h + 1) * HALF) for h in range(HALVES)]
-            for cols in halves:
+            last["tiles"] = (grouped_last, codes, scales, z_sb)
+
+        def regroup_last(h, engine):
+            cols = slice(h * HALF, (h + 1) * HALF)
+            engine.tensor_scalar(
+                out=last["tiles"][0][:, cols, :],
+                in0=planes[LAST][:, :, cols].rearrange("m t n -> m n t"),
+                scalar1=1.0,
+                scalar2=0.0,
+                op0=ALU.mult,
+                op1=ALU.add,
+            )
+
+        def quantise_last(h):
+            cols = slice(h * HALF, (h + 1) * HALF)
+            side_by_side, codes, scales, z_sb = last["tiles"]
+            nc.vector.quantize_mx(
+                out=codes[:, cols].bitcast(FP8X4),
+                scales=scales[:, cols],
+                in_=side_by_side[:, cols, :].rearrange("m n t -> m (n t)"),
+            )
+
+        def multiply_last(h, tags):
+            cols = slice(h * HALF, (h + 1) * HALF)
+            side_by_side, codes, scales, z_sb = last["tiles"]
+            for t in range(OUT_TILES):
+                o_cols = slice(t * P, (t + 1) * P)
+                acc = psum.tile([P, HALF], F32, tag=tags[t])
+                nc.tensor.matmul_mx(
+                    out=acc[:],
+                    lhsT=w_codes[:, o_cols].bitcast(FP8X4),
+                    lhsT_scale=w_scales[:, o_cols],
+                    rhs=codes[:, cols].bitcast(FP8X4),
+                    rhs_scale=scales[:, cols],
+                    start=True,
+                    stop=True,
+                )
+                last[h, t] = acc
+
+        def finish_last(h, t, on_scalar):
+            cols = slice(h * HALF, (h + 1) * HALF)
+            z_sb = last["tiles"][3]
+            acc = last[h, t]
+            if on_scalar:
+                nc.scalar.activation(
+                    out=z_sb[:, t, cols], in_=acc[:], func=ACT.Identity, bias=bias[:, t : t + 1]
+                )
+            else:
                 nc.vector.tensor_scalar(
-                    out=side_by_side[:, cols, :],
-                    in0=planes[b][:, :, cols].rearrange("m t n -> m n t"),
-                    scalar1=1.0,
-                    scalar2=0.0,
-                    op0=ALU.mult,
-                    op1=ALU.add,
+                    out=z_sb[:, t, cols],
+                    in0=acc[:],
+                    scalar1=bias[:, t : t + 1],
+                    scalar2=None,
+                    op0=ALU.add,
                 )
-            for cols in halves:
-                nc.vector.quantize_mx(
-                    out=codes[:, cols].bitcast(FP8X4),
-                    scales=scales[:, cols],
-                    in_=side_by_side[:, cols, :].rearrange("m n t -> m (n t)"),
-                )
-            for cols in halves:
-                for t in range(OUT_TILES):
-                    o_cols = slice(t * P, (t + 1) * P)
-                    acc = psum.tile([P, HALF], F32, tag=("acc", "x1t", "x2t", "x3t")[t])
-                    nc.tensor.matmul_mx(
-                        out=acc[:],
-                        lhsT=w_codes[:, o_cols].bitcast(FP8X4),
-                        lhsT_scale=w_scales[:, o_cols],
-                        rhs=codes[:, cols].bitcast(FP8X4),
-                        rhs_scale=scales[:, cols],
-                        start=True,
-                        stop=True,
-                    )
-                    if t % 2 == 0:
-                        nc.scalar.activation(
-                            out=z_sb[:, t, cols], in_=acc[:], func=ACT.Identity, bias=bias[:, t : t + 1]
-                        )
-                    else:
-                        nc.vector.tensor_scalar(
-                            out=z_sb[:, t, cols],
-                            in0=acc[:],
-                            scalar1=bias[:, t : t + 1],
-                            scalar2=None,
-                            op0=ALU.add,
-                        )
-                    nc.sync.dma_start(out=z_dram[b][:, t, cols], in_=z_sb[:, t, cols])
+            nc.sync.dma_start(out=z_dram[LAST][:, t, cols], in_=z_sb[:, t, cols])
 
         for k in range(BRANCHES):
             for s in range(AHEAD):
@@ -306,7 +339,7 @@ def tile_modelnew_pb_t_kernel(tc, x1, x2, x3, hat, w2_words, w2_scales, b2, out)
             if ahead < STEPS:
                 transpose_map(0, ahead)
                 start_sum(ahead)
-            add_second(s)
+            add_second(s, 0)
             if ahead < STEPS:
                 transpose_map(1, ahead)
 
@@ -314,7 +347,10 @@ def tile_modelnew_pb_t_kernel(tc, x1, x2, x3, hat, w2_words, w2_scales, b2, out)
             ahead = s + AHEAD
             second_step = s % PAIRS == 1
             if second_step and s > PAIRS:
-                project(s // PAIRS - 1)
+                quantise(s // PAIRS - 1)
+                project(s // PAIRS - 1, (0, 1))
+            if not second_step and s >= 2 * PAIRS:
+                project(s // PAIRS - 2, (2, 3))
             add_third(s)
             if ahead < STEPS:
                 transpose_map(2, ahead)
@@ -325,7 +361,29 @@ def tile_modelnew_pb_t_kernel(tc, x1, x2, x3, hat, w2_words, w2_scales, b2, out)
             first_half(s)
         for s in range(PAIRS):
             second_half(s)
-        for s in range(PAIRS, STEPS):
+        for s in range(PAIRS, STEPS - PAIRS):
             first_half(s)
             second_half(s)
-        project_last()
+        first, second = STEPS - PAIRS, STEPS - 1
+        last_tiles()
+        add_second(first, 0)
+        add_second(first, 1)
+        project(LAST - 2, (2, 3))
+        add_third(first)
+        regroup_last(0, nc.gpsimd)
+        add_second(second, 0)
+        quantise(LAST - 1)
+        project(LAST - 1, range(OUT_TILES))
+        add_second(second, 1)
+        quantise_last(0)
+        add_third(second)
+        multiply_last(0, ("x2t", "x2t", "acc", "acc"))
+        finish_last(0, 0, False)
+        regroup_last(1, nc.vector)
+        finish_last(0, 1, False)
+        quantise_last(1)
+        finish_last(0, 2, True)
+        finish_last(0, 3, True)
+        multiply_last(1, ("x3t", "x3t", "x1t", "x1t"))
+        for t in range(OUT_TILES):
+            finish_last(1, t, t % 2 == 1)

@@ -25,7 +25,9 @@ PAIRS = 2
 OUT_TILES = CH // P
 STEPS = BATCH * PAIRS
 AHEAD = 2
+SPLIT = (0, BATCH - 1)
 LAST = BATCH - 1
+FIRST_ORDER = ((0, 0), (1, 0), (0, 1), (1, 1), (2, 0), (2, 1))
 HALVES = 2
 HALF = POS // HALVES
 
@@ -62,8 +64,16 @@ def tile_modelnew_pb_t_kernel(tc, x1, x2, x3, hat, w2_words, w2_scales, b2, out)
         nc.sync.dma_start(out=hat_rows[16:HAT_ROWS, :], in_=hat_dram[16:HAT_ROWS, :])
         nc.sync.dma_start(out=hat_rows[HAT_ROWS:32, :], in_=hat_dram[0 : 32 - HAT_ROWS, :])
         x_sb = {}
+        for k in range(BRANCHES):
+            x_sb[k, 0] = resident.tile([P, ROWS * CH], BF16, name="x%d_b0" % (k + 1))
+        half_row = ROWS * CH // HALVES
+        for k, h in FIRST_ORDER:
+            cols = slice(h * half_row, (h + 1) * half_row)
+            nc.sync.dma_start(out=x_sb[k, 0][:, cols], in_=maps[k][0][:, cols])
         for b in range(BATCH):
             for k in range(BRANCHES):
+                if b == 0:
+                    continue
                 x_sb[k, b] = resident.tile([P, ROWS * CH], BF16, name="x%d_b%d" % (k + 1, b))
                 if b < LAST:
                     nc.sync.dma_start(out=x_sb[k, b][:], in_=maps[k][b])
@@ -145,7 +155,7 @@ def tile_modelnew_pb_t_kernel(tc, x1, x2, x3, hat, w2_words, w2_scales, b2, out)
 
         def parts_of(s):
             b, h = divmod(s, PAIRS)
-            if b < LAST:
+            if b not in SPLIT:
                 return [(h, 0, slice(0, POS))]
             return [(u, u * HALF, slice(h * HALF, (h + 1) * HALF)) for u in range(PAIRS)]
 
@@ -154,7 +164,7 @@ def tile_modelnew_pb_t_kernel(tc, x1, x2, x3, hat, w2_words, w2_scales, b2, out)
             words = x_sb[k, b][:].bitcast(F32)
             bank = psum.tile([P, ROWS, P], F32, tag="x%dt" % (k + 1))
             for i in range(ROWS):
-                u, j = (h, i) if b < LAST else (i // 2, h * 2 + i % 2)
+                u, j = (i // 2, h * 2 + i % 2) if b in SPLIT else (h, i)
                 first = j * (CH // 2) + u
                 nc.tensor.transpose(
                     bank[:, i, :], words[:, first : (j + 1) * (CH // 2) : PAIRS], ident[:]
@@ -324,9 +334,8 @@ def tile_modelnew_pb_t_kernel(tc, x1, x2, x3, hat, w2_words, w2_scales, b2, out)
                 )
             nc.sync.dma_start(out=z_dram[LAST][:, t, cols], in_=z_sb[:, t, cols])
 
-        for k in range(BRANCHES):
-            for s in range(AHEAD):
-                transpose_map(k, s)
+        for k, s in FIRST_ORDER:
+            transpose_map(k, s)
         for s in range(AHEAD):
             start_sum(s)
         b2_f32 = const.tile([P, P], F32)
@@ -339,7 +348,8 @@ def tile_modelnew_pb_t_kernel(tc, x1, x2, x3, hat, w2_words, w2_scales, b2, out)
             if ahead < STEPS:
                 transpose_map(0, ahead)
                 start_sum(ahead)
-            add_second(s, 0)
+            for part in range(len(parts_of(s))):
+                add_second(s, part)
             if ahead < STEPS:
                 transpose_map(1, ahead)
 

@@ -28,6 +28,8 @@ AHEAD = 2
 SPLIT = (0, BATCH - 1)
 LAST = BATCH - 1
 FIRST_ORDER = ((0, 0), (1, 0), (0, 1), (1, 1), (2, 0), (2, 1))
+PRODUCT_BANKS = {LAST - 2: ("acc", "acc", "x1t", "x1t"), LAST - 1: ("acc", "acc", "x2t", "x1t")}
+LAST_BANKS = (("x3t", "x2t", "x1t", "acc"), ("x3t", "acc", "x2t", "x3t"))
 HALVES = 2
 HALF = POS // HALVES
 
@@ -109,42 +111,56 @@ def tile_modelnew_pb_t_kernel(tc, x1, x2, x3, hat, w2_words, w2_scales, b2, out)
             .bitcast(BF16)
             .rearrange("m (g k e) -> m g k e", k=BRANCHES, e=2)
         )
+        first_groups = slice(0, groups, BATCH)
+        low = const.tile([P, PAIRS, 2], F32)
+        first_exp = const.tile([P, PAIRS, BRANCHES, 2], F32)
+        first_total = const.tile([P, PAIRS, 2], F32)
+        first_gate = const.tile([P, PAIRS, BRANCHES, 2], F32)
         top = const.tile([P, groups, 2], F32)
         logits = const.tile([P, groups, BRANCHES, 2], F32)
         expd = const.tile([P, groups, BRANCHES, 2], F32)
         total = const.tile([P, groups, 2], F32)
         gate = const.tile([P, groups, BRANCHES, 2], F32)
-        parts = (slice(0, 1), slice(1, groups))
 
-        def over_branches(per_group, g):
-            return per_group[:, g, :].unsqueeze(2).to_broadcast([P, g.stop - g.start, BRANCHES, 2])
+        def over_branches(per_group, count):
+            return per_group[:].unsqueeze(2).to_broadcast([P, count, BRANCHES, 2])
 
-        for g in parts:
-            nc.vector.tensor_reduce(
-                out=top[:, g, :],
-                in_=raw_logits[:, g, :, :].rearrange("m g k e -> m g e k"),
-                axis=AXIS.X,
-                op=ALU.max,
-            )
-        for g in parts:
-            nc.vector.tensor_sub(
-                out=logits[:, g, :, :], in0=raw_logits[:, g, :, :], in1=over_branches(top, g)
-            )
-        for g in parts:
-            nc.scalar.activation(out=expd[:, g, :, :], in_=logits[:, g, :, :], func=ACT.Exp)
-        for g in parts:
-            nc.vector.tensor_reduce(
-                out=total[:, g, :],
-                in_=expd[:, g, :, :].rearrange("m g k e -> m g e k"),
-                axis=AXIS.X,
-                op=ALU.add,
-            )
-        for g in parts:
-            nc.vector.reciprocal(out=total[:, g, :], in_=total[:, g, :])
-        for g in parts:
-            nc.vector.tensor_mul(
-                out=gate[:, g, :, :], in0=expd[:, g, :, :], in1=over_branches(total, g)
-            )
+        nc.vector.tensor_reduce(
+            out=low[:],
+            in_=raw_logits[:, first_groups, :, :].rearrange("m g k e -> m g e k"),
+            axis=AXIS.X,
+            op=ALU.max,
+            negate=True,
+        )
+        nc.vector.tensor_reduce(
+            out=top[:],
+            in_=raw_logits.rearrange("m g k e -> m g e k"),
+            axis=AXIS.X,
+            op=ALU.max,
+        )
+        for u in range(PAIRS):
+            for e in range(2):
+                nc.scalar.activation(
+                    out=first_exp[:, u, :, e],
+                    in_=raw_logits[:, u * BATCH, :, e],
+                    func=ACT.Exp,
+                    bias=low[:, u, e : e + 1],
+                    accum_out=first_total[:, u, e : e + 1],
+                )
+        nc.vector.tensor_sub(out=logits[:], in0=raw_logits, in1=over_branches(top, groups))
+        nc.vector.reciprocal(out=first_total[:], in_=first_total[:])
+        nc.vector.tensor_mul(
+            out=first_gate[:], in0=first_exp[:], in1=over_branches(first_total, PAIRS)
+        )
+        nc.scalar.activation(out=expd[:], in_=logits[:], func=ACT.Exp)
+        nc.vector.tensor_reduce(
+            out=total[:],
+            in_=expd[:].rearrange("m g k e -> m g e k"),
+            axis=AXIS.X,
+            op=ALU.add,
+        )
+        nc.vector.reciprocal(out=total[:], in_=total[:])
+        nc.vector.tensor_mul(out=gate[:], in0=expd[:], in1=over_branches(total, groups))
 
         bias = const.tile([P, OUT_TILES], F32)
 
@@ -176,6 +192,8 @@ def tile_modelnew_pb_t_kernel(tc, x1, x2, x3, hat, w2_words, w2_scales, b2, out)
             return halves.rearrange("m (n e) -> m n e", e=2)[:, start : start + count, e]
 
         def weight(k, b, u, e):
+            if b == 0:
+                return first_gate[:, u, k, e : e + 1]
             return gate[:, u * BATCH + b, k, e : e + 1]
 
         def start_sum(s):
@@ -205,13 +223,13 @@ def tile_modelnew_pb_t_kernel(tc, x1, x2, x3, hat, w2_words, w2_scales, b2, out)
                     op1=ALU.add,
                 )
 
-        def add_third(s):
+        def add_third(s, parts=slice(None)):
             b, h = divmod(s, PAIRS)
-            if h == 0:
+            if b not in planes:
                 plane = work.tile([P, PACK, POS], BF16)
                 planes[b] = plane
             partial = partials[s]
-            for u, start, cols in parts_of(s):
+            for u, start, cols in parts_of(s)[parts]:
                 count = cols.stop - cols.start
                 for e in range(2):
                     nc.vector.scalar_tensor_tensor(
@@ -252,7 +270,7 @@ def tile_modelnew_pb_t_kernel(tc, x1, x2, x3, hat, w2_words, w2_scales, b2, out)
             codes, scales, z_sb = quantised[b]
             for t in tiles:
                 o_cols = slice(t * P, (t + 1) * P)
-                acc = psum.tile([P, POS], F32, tag="x1t" if b == LAST - 1 and t >= 2 else "acc")
+                acc = psum.tile([P, POS], F32, tag=PRODUCT_BANKS.get(b, ("acc",) * OUT_TILES)[t])
                 nc.tensor.matmul_mx(
                     out=acc[:],
                     lhsT=w_codes[:, o_cols].bitcast(FP8X4),
@@ -299,12 +317,12 @@ def tile_modelnew_pb_t_kernel(tc, x1, x2, x3, hat, w2_words, w2_scales, b2, out)
                 in_=side_by_side[:, cols, :].rearrange("m n t -> m (n t)"),
             )
 
-        def multiply_last(h, tags):
+        def multiply_last(h):
             cols = slice(h * HALF, (h + 1) * HALF)
             side_by_side, codes, scales, z_sb = last["tiles"]
             for t in range(OUT_TILES):
                 o_cols = slice(t * P, (t + 1) * P)
-                acc = psum.tile([P, HALF], F32, tag=tags[t])
+                acc = psum.tile([P, HALF], F32, tag=LAST_BANKS[h][t])
                 nc.tensor.matmul_mx(
                     out=acc[:],
                     lhsT=w_codes[:, o_cols].bitcast(FP8X4),
@@ -385,15 +403,16 @@ def tile_modelnew_pb_t_kernel(tc, x1, x2, x3, hat, w2_words, w2_scales, b2, out)
         quantise(LAST - 1)
         project(LAST - 1, range(OUT_TILES))
         add_second(second, 1)
+        add_third(second, slice(0, 1))
         quantise_last(0)
-        add_third(second)
-        multiply_last(0, ("x2t", "x2t", "acc", "acc"))
-        finish_last(0, 0, False)
+        add_third(second, slice(1, 2))
+        multiply_last(0)
         regroup_last(1, nc.vector)
-        finish_last(0, 1, False)
+        finish_last(0, 0, False)
         quantise_last(1)
-        finish_last(0, 2, True)
+        finish_last(0, 1, False)
+        finish_last(0, 2, False)
         finish_last(0, 3, True)
-        multiply_last(1, ("x3t", "x3t", "x1t", "x1t"))
+        multiply_last(1)
         for t in range(OUT_TILES):
             finish_last(1, t, t % 2 == 1)

from contextlib import ExitStack

import concourse.mybir as mybir
from concourse.masks import make_identity

F32 = mybir.dt.float32
BF16 = mybir.dt.bfloat16
I32 = mybir.dt.int32
U32 = mybir.dt.uint32
U8 = mybir.dt.uint8
FP8X4 = mybir.dt.float8_e4m3fn_x4
ACT = mybir.ActivationFunctionType
ALU = mybir.AluOpType
AXIS = mybir.AxisListType

P = 128
PACK = 4
BATCH = 8
POS = 512
CH = 512
BRANCHES = 3
HAT_ROWS = BATCH * BRANCHES
ROWS = POS // P
PAIRS = 2
OUT_TILES = CH // P
STEPS = BATCH * PAIRS
AHEAD = 2
SPLIT = (0, BATCH - 1)
LAST = BATCH - 1
FIRST_ORDER = ((0, 0), (1, 0), (0, 1), (1, 1), (2, 0), (2, 1))
PRODUCT_BANKS = {LAST - 2: ("acc", "acc", "x1t", "x1t"), LAST - 1: ("acc", "acc", "x2t", "x1t")}
LAST_BANKS = (("x3t", "x2t", "x1t", "acc"), ("x3t", "acc", "x2t", "x3t"))
HALVES = 2
HALF = POS // HALVES

FLOPS = 2 * BATCH * POS * CH * CH


def tile_modelnew_pb_t_kernel(tc, x1, x2, x3, hat, w2_words, w2_scales, b2, out):
    nc = tc.nc
    maps = [x.rearrange("b w (g j) c -> b (w g) (j c)", j=ROWS) for x in (x1, x2, x3)]
    z_dram = out.rearrange("b (t o) w h -> b o t (w h)", o=P)

    with ExitStack() as ctx:
        ctx.enter_context(tc.manual_schedule())
        const = ctx.enter_context(tc.tile_pool(name="const", bufs=1))
        resident = ctx.enter_context(tc.tile_pool(name="resident", bufs=1))
        sums = ctx.enter_context(tc.tile_pool(name="sums", bufs=4))
        work = ctx.enter_context(tc.tile_pool(name="work", bufs=2))
        results = ctx.enter_context(tc.tile_pool(name="results", bufs=BATCH))
        psum = ctx.enter_context(tc.psum_pool(name="psum", bufs=2))

        ident = const.tile([P, P], F32)
        make_identity(nc, ident[:])
        hat_rows = const.tile([P, CH], BF16)
        nc.vector.memset(hat_rows[32:64, :], 0.0)
        nc.vector.memset(hat_rows[64:128, :], 0.0)
        b2_rows = const.tile([P, P], BF16)
        nc.gpsimd.memset(b2_rows[:], 0.0)
        w_scales = const.tile([P, CH], U8, align_bytes=64)
        nc.vector.memset(w_scales[:].bitcast(I32), 0)
        w_codes = const.tile([P, CH], U32, align_bytes=64)

        hat_dram = hat.rearrange("b (k c) -> (b k) c", k=BRANCHES)
        nc.sync.dma_start(out=hat_rows[0:16, :], in_=hat_dram[0:16, :])
        nc.sync.dma_start(out=hat_rows[16:HAT_ROWS, :], in_=hat_dram[16:HAT_ROWS, :])
        nc.sync.dma_start(out=hat_rows[HAT_ROWS:32, :], in_=hat_dram[0 : 32 - HAT_ROWS, :])
        x_sb = {}
        for k in range(BRANCHES):
            x_sb[k, 0] = resident.tile([P, ROWS * CH], BF16, name="x%d_b0" % (k + 1))
        half_row = ROWS * CH // HALVES
        for k, h in FIRST_ORDER:
            cols = slice(h * half_row, (h + 1) * half_row)
            nc.sync.dma_start(out=x_sb[k, 0][:, cols], in_=maps[k][0][:, cols])
        for b in range(BATCH):
            for k in range(BRANCHES):
                if b == 0:
                    continue
                x_sb[k, b] = resident.tile([P, ROWS * CH], BF16, name="x%d_b%d" % (k + 1, b))
                if b < LAST:
                    nc.sync.dma_start(out=x_sb[k, b][:], in_=maps[k][b])
                else:
                    nc.sync.dma_start(
                        out=x_sb[k, b][:].rearrange("q (j c) -> q j c", j=ROWS),
                        in_=(x1, x2, x3)[k][b].rearrange("(j v) h c -> (v h) j c", j=ROWS),
                    )
            if b == 0:
                nc.sync.dma_start(
                    out=b2_rows[0:OUT_TILES, :], in_=b2.rearrange("(t o) -> t o", o=P)
                )
            if b == 1:
                nc.sync.dma_start(
                    out=w_codes[:].bitcast(I32),
                    in_=w2_words[0].rearrange("p n t -> p (n t)").bitcast(I32),
                )
                for quad in range(4):
                    nc.sync.dma_start(
                        out=w_scales[32 * quad : 32 * quad + 4, :].bitcast(I32),
                        in_=w2_scales[0, 4 * quad : 4 * quad + 4, :].bitcast(I32),
                    )

        hat_words = hat_rows[:].bitcast(F32)
        hat_t = psum.tile([P, HAT_ROWS + P], F32, tag="acc")
        for u in range(PAIRS):
            nc.tensor.transpose(
                hat_t[:, u * HAT_ROWS : u * HAT_ROWS + P], hat_words[:, u : CH // 2 : PAIRS], ident[:]
            )
        groups = PAIRS * BATCH
        raw_logits = (
            hat_t[:, 0 : PAIRS * HAT_ROWS]
            .bitcast(BF16)
            .rearrange("m (g k e) -> m g k e", k=BRANCHES, e=2)
        )
        first_groups = slice(0, groups, BATCH)
        low = const.tile([P, PAIRS, 2], F32)
        first_exp = const.tile([P, PAIRS, BRANCHES, 2], F32)
        first_total = const.tile([P, PAIRS, 2], F32)
        first_gate = const.tile([P, PAIRS, BRANCHES, 2], F32)
        top = const.tile([P, groups, 2], F32)
        logits = const.tile([P, groups, BRANCHES, 2], F32)
        expd = const.tile([P, groups, BRANCHES, 2], F32)
        total = const.tile([P, groups, 2], F32)
        gate = const.tile([P, groups, BRANCHES, 2], F32)

        def over_branches(per_group, count):
            return per_group[:].unsqueeze(2).to_broadcast([P, count, BRANCHES, 2])

        nc.vector.tensor_reduce(
            out=low[:],
            in_=raw_logits[:, first_groups, :, :].rearrange("m g k e -> m g e k"),
            axis=AXIS.X,
            op=ALU.max,
            negate=True,
        )
        nc.vector.tensor_reduce(
            out=top[:],
            in_=raw_logits.rearrange("m g k e -> m g e k"),
            axis=AXIS.X,
            op=ALU.max,
        )
        for u in range(PAIRS):
            for e in range(2):
                nc.scalar.activation(
                    out=first_exp[:, u, :, e],
                    in_=raw_logits[:, u * BATCH, :, e],
                    func=ACT.Exp,
                    bias=low[:, u, e : e + 1],
                    accum_out=first_total[:, u, e : e + 1],
                )
        nc.vector.tensor_sub(out=logits[:], in0=raw_logits, in1=over_branches(top, groups))
        nc.vector.reciprocal(out=first_total[:], in_=first_total[:])
        nc.vector.tensor_mul(
            out=first_gate[:], in0=first_exp[:], in1=over_branches(first_total, PAIRS)
        )
        nc.scalar.activation(out=expd[:], in_=logits[:], func=ACT.Exp)
        nc.vector.tensor_reduce(
            out=total[:],
            in_=expd[:].rearrange("m g k e -> m g e k"),
            axis=AXIS.X,
            op=ALU.add,
        )
        nc.vector.reciprocal(out=total[:], in_=total[:])
        nc.vector.tensor_mul(out=gate[:], in0=expd[:], in1=over_branches(total, groups))

        bias = const.tile([P, OUT_TILES], F32)

        banks = {}
        partials = {}
        planes = {}
        grouped = {}

        def parts_of(s):
            b, h = divmod(s, PAIRS)
            if b not in SPLIT:
                return [(h, 0, slice(0, POS))]
            return [(u, u * HALF, slice(h * HALF, (h + 1) * HALF)) for u in range(PAIRS)]

        def transpose_map(k, s):
            b, h = divmod(s, PAIRS)
            words = x_sb[k, b][:].bitcast(F32)
            bank = psum.tile([P, ROWS, P], F32, tag="x%dt" % (k + 1))
            for i in range(ROWS):
                u, j = (i // 2, h * 2 + i % 2) if b in SPLIT else (h, i)
                first = j * (CH // 2) + u
                nc.tensor.transpose(
                    bank[:, i, :], words[:, first : (j + 1) * (CH // 2) : PAIRS], ident[:]
                )
            banks[k, s] = bank

        def channel_of_pair(k, s, e, start, count):
            halves = banks[k, s][:].rearrange("m j q -> m (j q)").bitcast(BF16)
            return halves.rearrange("m (n e) -> m n e", e=2)[:, start : start + count, e]

        def weight(k, b, u, e):
            if b == 0:
                return first_gate[:, u, k, e : e + 1]
            return gate[:, u * BATCH + b, k, e : e + 1]

        def start_sum(s):
            partial = sums.tile([P, 2, POS], F32)
            for u, start, cols in parts_of(s):
                count = cols.stop - cols.start
                for e in range(2):
                    nc.scalar.activation(
                        out=partial[:, e, start : start + count],
                        in_=channel_of_pair(0, s, e, start, count),
                        func=ACT.Copy,
                        scale=weight(0, s // PAIRS, u, e),
                    )
            partials[s] = partial

        def add_second(s, part):
            partial = partials[s]
            u, start, cols = parts_of(s)[part]
            count = cols.stop - cols.start
            for e in range(2):
                nc.vector.scalar_tensor_tensor(
                    out=partial[:, e, start : start + count],
                    in0=channel_of_pair(1, s, e, start, count),
                    scalar=weight(1, s // PAIRS, u, e),
                    in1=partial[:, e, start : start + count],
                    op0=ALU.mult,
                    op1=ALU.add,
                )

        def add_third(s, parts=slice(None)):
            b, h = divmod(s, PAIRS)
            if b not in planes:
                plane = work.tile([P, PACK, POS], BF16)
                planes[b] = plane
            partial = partials[s]
            for u, start, cols in parts_of(s)[parts]:
                count = cols.stop - cols.start
                for e in range(2):
                    nc.vector.scalar_tensor_tensor(
                        out=planes[b][:, 2 * u + e, cols],
                        in0=channel_of_pair(2, s, e, start, count),
                        scalar=weight(2, b, u, e),
                        in1=partial[:, e, start : start + count],
                        op0=ALU.mult,
                        op1=ALU.add,
                    )

        def regroup(b):
            side_by_side = work.tile([P, POS, PACK], BF16, align_bytes=64)
            nc.gpsimd.tensor_scalar(
                out=side_by_side[:],
                in0=planes[b][:].rearrange("m t n -> m n t"),
                scalar1=1.0,
                scalar2=0.0,
                op0=ALU.mult,
                op1=ALU.add,
            )
            grouped[b] = side_by_side

        quantised = {}

        def quantise(b):
            codes = work.tile([P, POS], U32, align_bytes=64)
            scales = work.tile([P, POS], U8, align_bytes=64)
            nc.vector.quantize_mx(
                out=codes[:].bitcast(FP8X4),
                scales=scales[:],
                in_=grouped[b][:].rearrange("m n t -> m (n t)"),
            )
            z_sb = results.tile([P, OUT_TILES, POS], F32)
            quantised[b] = (codes, scales, z_sb)

        def project(b, tiles):
            codes, scales, z_sb = quantised[b]
            for t in tiles:
                o_cols = slice(t * P, (t + 1) * P)
                acc = psum.tile([P, POS], F32, tag=PRODUCT_BANKS.get(b, ("acc",) * OUT_TILES)[t])
                nc.tensor.matmul_mx(
                    out=acc[:],
                    lhsT=w_codes[:, o_cols].bitcast(FP8X4),
                    lhsT_scale=w_scales[:, o_cols],
                    rhs=codes[:].bitcast(FP8X4),
                    rhs_scale=scales[:],
                    start=True,
                    stop=True,
                )
                nc.scalar.activation(
                    out=z_sb[:, t, :].rearrange("o (q j) -> o q j", j=ROWS),
                    in_=acc[:].rearrange("o (j q) -> o q j", j=ROWS),
                    func=ACT.Identity,
                    bias=bias[:, t : t + 1],
                )
                nc.sync.dma_start(out=z_dram[b][:, t, :], in_=z_sb[:, t, :])

        last = {}

        def last_tiles():
            grouped_last = work.tile([P, POS, PACK], BF16, align_bytes=64)
            codes = work.tile([P, POS], U32, align_bytes=64)
            scales = work.tile([P, POS], U8, align_bytes=64)
            z_sb = results.tile([P, OUT_TILES, POS], F32)
            last["tiles"] = (grouped_last, codes, scales, z_sb)

        def regroup_last(h, engine):
            cols = slice(h * HALF, (h + 1) * HALF)
            engine.tensor_scalar(
                out=last["tiles"][0][:, cols, :],
                in0=planes[LAST][:, :, cols].rearrange("m t n -> m n t"),
                scalar1=1.0,
                scalar2=0.0,
                op0=ALU.mult,
                op1=ALU.add,
            )

        def quantise_last(h):
            cols = slice(h * HALF, (h + 1) * HALF)
            side_by_side, codes, scales, z_sb = last["tiles"]
            nc.vector.quantize_mx(
                out=codes[:, cols].bitcast(FP8X4),
                scales=scales[:, cols],
                in_=side_by_side[:, cols, :].rearrange("m n t -> m (n t)"),
            )

        def multiply_last(h):
            cols = slice(h * HALF, (h + 1) * HALF)
            side_by_side, codes, scales, z_sb = last["tiles"]
            for t in range(OUT_TILES):
                o_cols = slice(t * P, (t + 1) * P)
                acc = psum.tile([P, HALF], F32, tag=LAST_BANKS[h][t])
                nc.tensor.matmul_mx(
                    out=acc[:],
                    lhsT=w_codes[:, o_cols].bitcast(FP8X4),
                    lhsT_scale=w_scales[:, o_cols],
                    rhs=codes[:, cols].bitcast(FP8X4),
                    rhs_scale=scales[:, cols],
                    start=True,
                    stop=True,
                )
                last[h, t] = acc

        def finish_last(h, t, on_scalar):
            cols = slice(h * HALF, (h + 1) * HALF)
            z_sb = last["tiles"][3]
            acc = last[h, t]
            if on_scalar:
                nc.scalar.activation(
                    out=z_sb[:, t, cols], in_=acc[:], func=ACT.Identity, bias=bias[:, t : t + 1]
                )
            else:
                nc.vector.tensor_scalar(
                    out=z_sb[:, t, cols],
                    in0=acc[:],
                    scalar1=bias[:, t : t + 1],
                    scalar2=None,
                    op0=ALU.add,
                )
            nc.sync.dma_start(out=z_dram[LAST][:, t, cols], in_=z_sb[:, t, cols])

        for k, s in FIRST_ORDER:
            transpose_map(k, s)
        for s in range(AHEAD):
            start_sum(s)
        b2_f32 = const.tile([P, P], F32)
        nc.gpsimd.tensor_copy(out=b2_f32[:], in_=b2_rows[:])
        b2_t = psum.tile([P, P], F32, tag="acc")
        nc.tensor.transpose(b2_t[:], b2_f32[:], ident[:])
        nc.scalar.copy(out=bias[:], in_=b2_t[:, 0:OUT_TILES])
        def first_half(s):
            ahead = s + AHEAD
            if ahead < STEPS:
                transpose_map(0, ahead)
                start_sum(ahead)
            for part in range(len(parts_of(s))):
                add_second(s, part)
            if ahead < STEPS:
                transpose_map(1, ahead)

        def second_half(s):
            ahead = s + AHEAD
            second_step = s % PAIRS == 1
            if second_step and s > PAIRS:
                quantise(s // PAIRS - 1)
                project(s // PAIRS - 1, (0, 1))
            if not second_step and s >= 2 * PAIRS:
                project(s // PAIRS - 2, (2, 3))
            add_third(s)
            if ahead < STEPS:
                transpose_map(2, ahead)
            if second_step and s < STEPS - 1:
                regroup(s // PAIRS)

        for s in range(PAIRS):
            first_half(s)
        for s in range(PAIRS):
            second_half(s)
        for s in range(PAIRS, STEPS - PAIRS):
            first_half(s)
            second_half(s)
        first, second = STEPS - PAIRS, STEPS - 1
        last_tiles()
        add_second(first, 0)
        add_second(first, 1)
        project(LAST - 2, (2, 3))
        add_third(first)
        regroup_last(0, nc.gpsimd)
        add_second(second, 0)
        quantise(LAST - 1)
        project(LAST - 1, range(OUT_TILES))
        add_second(second, 1)
        add_third(second, slice(0, 1))
        quantise_last(0)
        add_third(second, slice(1, 2))
        multiply_last(0)
        regroup_last(1, nc.vector)
        finish_last(0, 0, False)
        quantise_last(1)
        finish_last(0, 1, False)
        finish_last(0, 2, False)
        finish_last(0, 3, True)
        multiply_last(1)
        for t in range(OUT_TILES):
            finish_last(1, t, t % 2 == 1)
